import numpy as np
import ml_dtypes


def mxq(x, axis, fmt="e4m3"):
    dtype, down = {"e4m3": (ml_dtypes.float8_e4m3fn, 7), "e5m2": (ml_dtypes.float8_e5m2, 14)}[fmt]
    v = np.moveaxis(np.asarray(x, np.float32).astype(ml_dtypes.bfloat16).astype(np.float64), axis, -1)
    blocks = v.reshape(v.shape[:-1] + (-1, 32))
    amax = np.abs(blocks).max(-1, keepdims=True)
    byte = np.maximum(np.where(amax > 0, np.frexp(amax)[1] - 1 + 127, 0) - down, 1)
    scale = np.exp2(byte - 127.0)
    codes = (blocks / scale).astype(np.float32).astype(dtype).astype(np.float64)
    return np.moveaxis((codes * scale).reshape(v.shape), -1, axis)


WIDE = False


def mx_kscale(k):
    if not WIDE:
        return np.ones(k)
    levels = np.array([10, -10, 5, -5, 0])
    a = np.random.permutation(np.resize(levels, k // 512 * 4)).reshape(k // 512, 4)
    idx = np.arange(k)
    return np.exp2(a[idx // 512, idx % 128 // 32])


BF16 = ml_dtypes.bfloat16


def bf(x):
    return np.asarray(x, np.float32).astype(BF16)


def f64(x):
    return np.asarray(x).astype(np.float64)


B, H, L, D, DV = 1, 2, 2048, 128, 256


def setup_inputs():
    keep = (np.random.random((B, L, L)) < 0.75) | np.eye(L, dtype=bool)
    s = mx_kscale(L)
    q = np.random.standard_normal((B, H, L, D)) * 1.2
    k = np.random.standard_normal((B, H, L, D)) * 1.2
    v = np.random.standard_normal((B, H, L, DV))
    pe_q = np.random.standard_normal((B, H, L, D)) * 1.2
    pe_k = np.random.standard_normal((B, H, L, D)) * 1.2
    pe_q[..., 0] = 1.0
    pe_k[..., 0] += np.log(s) * np.sqrt(D)
    v = v / s[:, None] * s.mean()
    return {"q": bf(q), "k": bf(k), "v": bf(v), "pe_q": bf(pe_q), "pe_k": bf(pe_k), "mask": bf(keep)}


def reference(q, k, v, pe_q, pe_k, mask):
    scale = D ** (-0.5)
    attn = (f64(q) @ f64(k).transpose(0, 1, 3, 2) + f64(pe_q) @ f64(pe_k).transpose(0, 1, 3, 2)) * scale
    attn = np.where(f64(mask)[:, None, :, :] != 0.0, attn, -np.inf)
    e = np.exp(attn - attn.max(-1, keepdims=True))
    return (mxq(e, 3, "e4m3") @ mxq(f64(v), 2, "e4m3")) / e.sum(-1, keepdims=True)

@@ -1,0 +1,269 @@
+from contextlib import ExitStack
+
+import concourse.mybir as mybir
+from concourse.masks import make_identity
+
+F32 = mybir.dt.float32
+BF16 = mybir.dt.bfloat16
+U32 = mybir.dt.uint32
+U8 = mybir.dt.uint8
+FP8X4 = mybir.dt.float8_e4m3fn_x4
+ALU = mybir.AluOpType
+ACT = mybir.ActivationFunctionType
+AX = mybir.AxisListType
+
+P = 128
+H = 2
+L = 2048
+D = 128
+DV = 256
+NT = L // P
+NU = H * NT
+CH = 512
+NCH = L // CH
+SCALE = D ** -0.5
+BIG = 1.0e30
+
+FLOPS = 2 * H * L * L * (2 * D + DV)
+
+
+def tile_attention_kernel(tc, q, k, v, pe_q, pe_k, mask, out):
+    nc = tc.nc
+    with ExitStack() as ctx:
+        keep = ctx.enter_context(tc.tile_pool(name="keep", bufs=1))
+        wpool = ctx.enter_context(tc.tile_pool(name="wpool", bufs=3))
+        epool = ctx.enter_context(tc.tile_pool(name="epool", bufs=3))
+        gpool = ctx.enter_context(tc.tile_pool(name="gpool", bufs=2))
+        cpool = ctx.enter_context(tc.tile_pool(name="cpool", bufs=2))
+        opool = ctx.enter_context(tc.tile_pool(name="opool", bufs=3))
+        small = ctx.enter_context(tc.tile_pool(name="small", bufs=6))
+        ps_s = ctx.enter_context(tc.psum_pool(name="ps_s", bufs=4))
+        ps_x = ctx.enter_context(tc.psum_pool(name="ps_x", bufs=2))
+        ps_o = ctx.enter_context(tc.psum_pool(name="ps_o", bufs=1))
+        ps_p = ctx.enter_context(tc.psum_pool(name="ps_p", bufs=1))
+
+        ident = keep.tile([P, P], BF16, name="ident")
+        make_identity(nc, ident[:])
+
+        raw = {}
+        for h in range(H):
+            for nm in ("q", "pq", "k", "pk"):
+                raw[(nm, h)] = keep.tile([P, NT, D], BF16, name="raw_%s%d" % (nm, h))
+        qq = [keep.tile([P, 2, NT, P], BF16, name="qq%d" % h) for h in range(H)]
+        kk = [keep.tile([P, 2, L], BF16, name="kk%d" % h) for h in range(H)]
+        mb = [keep.tile([P, L], BF16, name="mb%d" % i) for i in range(NT)]
+        vraw = [keep.tile([P, NT, DV], BF16, name="vraw%d" % h) for h in range(H)]
+        vcodes = [keep.tile([P, NCH * DV], U32, name="vcodes%d" % h, align_bytes=64) for h in range(H)]
+        vscl = [keep.tile([P, NCH * DV], U8, name="vscl%d" % h, align_bytes=64) for h in range(H)]
+
+        def load_keys(nm, src, h, lo, hi):
+            nc.sync.dma_start(
+                out=raw[(nm, h)][:, lo:hi, :],
+                in_=src[0, h].rearrange("(t p) d -> p t d", p=P)[:, lo:hi, :],
+            )
+
+        def load_queries(nm, src, h):
+            nc.sync.dma_start(out=raw[(nm, h)][:], in_=src[0, h].rearrange("(p t) d -> p t d", t=NT))
+
+        def load_mask(i):
+            nc.sync.dma_start(out=mb[i][:], in_=mask[0].rearrange("(p t) c -> t p c", t=NT)[i])
+
+        def load_v(h):
+            nc.sync.dma_start(out=vraw[h][:], in_=v[0, h].rearrange("(c p) n -> p c n", p=P))
+
+        load_keys("k", k, 0, 0, 8)
+        load_keys("pk", pe_k, 0, 0, 8)
+        load_queries("q", q, 0)
+        load_queries("pq", pe_q, 0)
+        load_mask(0)
+        load_keys("k", k, 0, 8, NT)
+        load_keys("pk", pe_k, 0, 8, NT)
+        load_mask(1)
+        load_v(0)
+        load_mask(2)
+        load_mask(3)
+        load_keys("k", k, 1, 0, NT)
+        load_keys("pk", pe_k, 1, 0, NT)
+        load_mask(4)
+        load_queries("q", q, 1)
+        load_queries("pq", pe_q, 1)
+        load_mask(5)
+        load_v(1)
+        for i in range(6, NT):
+            load_mask(i)
+
+        def bias_from_mask(eng, i, lo, hi):
+            eng.tensor_scalar(
+                out=mb[i][:, lo:hi], in0=mb[i][:, lo:hi],
+                scalar1=-1.0, scalar2=-BIG, op0=ALU.add, op1=ALU.mult,
+            )
+
+        vg = {}
+
+        def regroup_v(h):
+            vg[h] = gpool.tile([P, NCH, DV, 4], BF16, tag="vg", name="vg", bufs=1, align_bytes=64)
+            for g in range(NCH):
+                nc.gpsimd.tensor_scalar(
+                    out=vg[h][:, g, :, :],
+                    in0=vraw[h][:, 4 * g:4 * g + 4, :].rearrange("p t n -> p n t"),
+                    scalar1=1.0, scalar2=0.0, op0=ALU.mult, op1=ALU.add,
+                )
+
+        def quantise_v(h):
+            nc.vector.quantize_mx(
+                out=vcodes[h][:].bitcast(FP8X4),
+                scales=vscl[h][:],
+                in_=vg[h][:].rearrange("p g n t -> p (g n t)"),
+            )
+
+        def flip(pool, tag, a, b, h, c, dst, copy):
+            bank = pool.tile([P, 8, P], BF16, tag=tag, name="flip")
+            for n in range(8):
+                src = raw[(a if n < 4 else b, h)]
+                nc.tensor.transpose(bank[:, n, :], src[:, 4 * c + n % 4, :], ident[:])
+            copy(out=dst, in_=bank[:].rearrange("p (x c) r -> p x (c r)", x=2))
+
+        def flip_keys(pool, tag, h, c, copy):
+            flip(pool, tag, "k", "pk", h, c, kk[h][:, :, CH * c:CH * (c + 1)], copy)
+
+        def flip_queries(pool, tag, h, c, copy):
+            dst = qq[h][:, :, 4 * c:4 * c + 4, :].rearrange("p x c r -> p x (c r)")
+            flip(pool, tag, "q", "pq", h, c, dst, copy)
+
+        st = {}
+
+        def scores(u):
+            h, i = divmod(u, NT)
+            banks = []
+            for j in range(NCH):
+                s = ps_s.tile([P, CH], F32, tag="s", name="s")
+                cols = slice(CH * j, CH * (j + 1))
+                nc.tensor.matmul(s[:], lhsT=qq[h][:, 0, i, :], rhs=kk[h][:, 0, cols], start=True, stop=False)
+                nc.tensor.matmul(s[:], lhsT=qq[h][:, 1, i, :], rhs=kk[h][:, 1, cols], start=False, stop=True)
+                banks.append(s)
+            st[("s", u)] = banks
+
+        def mask_and_min(u):
+            i = u % NT
+            w = wpool.tile([P, L], F32, tag="w", name="w")
+            for j in range(NCH):
+                cols = slice(CH * j, CH * (j + 1))
+                nc.vector.scalar_tensor_tensor(
+                    out=w[:, cols], in0=st[("s", u)][j][:], scalar=-SCALE, in1=mb[i][:, cols],
+                    op0=ALU.mult, op1=ALU.add,
+                )
+            wmin = small.tile([P, 1], F32, tag="wmin", name="wmin")
+            nc.vector.tensor_reduce(out=wmin[:], in_=w[:], axis=AX.X, op=ALU.min)
+            st[("w", u)] = w
+            st[("wmin", u)] = wmin
+
+        def exponent(u):
+            e = epool.tile([P, L], BF16, tag="e", name="e")
+            rs = small.tile([P, 1], F32, tag="rs", name="rs")
+            nc.scalar.activation(
+                out=e[:], in_=st[("w", u)][:], func=ACT.Exp, bias=st[("wmin", u)][:], scale=-1.0,
+                accum_out=rs[:],
+            )
+            st[("e", u)] = e
+            st[("rs", u)] = rs
+
+        def flip_e(u):
+            e = st[("e", u)]
+            banks = []
+            for b in range(2):
+                xt = ps_x.tile([P, 8, P], BF16, tag="xt", name="xt")
+                for n in range(8):
+                    c = 8 * b + n
+                    nc.tensor.transpose(xt[:, n, :], e[:, P * c:P * (c + 1)], ident[:])
+                banks.append(xt)
+            st[("xt", u)] = banks
+
+        def group_e(u):
+            gr = gpool.tile([P, NCH, P, 4], BF16, tag="gr", name="gr", align_bytes=64)
+            for b in range(2):
+                nc.scalar.copy(
+                    out=gr[:, 2 * b:2 * b + 2, :, :],
+                    in_=st[("xt", u)][b][:].rearrange("p (g t) r -> p g r t", t=4),
+                )
+            st[("gr", u)] = gr
+
+        def quantise_e(u):
+            codes = cpool.tile([P, NCH * P], U32, tag="codes", name="codes", align_bytes=64)
+            scl = cpool.tile([P, NCH * P], U8, tag="scl", name="scl", align_bytes=64)
+            nc.vector.quantize_mx(
+                out=codes[:].bitcast(FP8X4), scales=scl[:],
+                in_=st[("gr", u)][:].rearrange("p g r t -> p (g r t)"),
+            )
+            rinv = small.tile([P, 1], F32, tag="rinv", name="rinv")
+            nc.vector.reciprocal(rinv[:], st[("rs", u)][:])
+            st[("codes", u)] = codes
+            st[("scl", u)] = scl
+            st[("rinv", u)] = rinv
+
+        def weighted_sum(u):
+            h, i = divmod(u, NT)
+            o = ps_o.tile([P, DV], F32, tag="o", name="o")
+            for g in range(NCH):
+                nc.tensor.matmul_mx(
+                    out=o[:],
+                    lhsT=st[("codes", u)][:, P * g:P * (g + 1)].bitcast(FP8X4),
+                    lhsT_scale=st[("scl", u)][:, P * g:P * (g + 1)],
+                    rhs=vcodes[h][:, DV * g:DV * (g + 1)].bitcast(FP8X4),
+                    rhs_scale=vscl[h][:, DV * g:DV * (g + 1)],
+                    start=(g == 0), stop=(g == NCH - 1),
+                )
+            res = opool.tile([P, DV], F32, tag="res", name="res")
+            nc.scalar.activation(out=res[:], in_=o[:], func=ACT.Copy, scale=st[("rinv", u)][:])
+            nc.sync.dma_start(out=out[0, h].rearrange("(p t) n -> t p n", t=NT)[i], in_=res[:])
+
+        vcopy = nc.vector.tensor_copy
+        scopy = nc.scalar.copy
+        flip_queries(ps_x, "xt", 0, 0, vcopy)
+        flip_keys(ps_s, "s", 0, 0, scopy)
+        for j in range(NCH):
+            bias_from_mask(nc.vector, 0, CH * j, CH * (j + 1))
+        flip_keys(ps_s, "s", 0, 1, vcopy)
+        flip_keys(ps_s, "s", 0, 2, scopy)
+        flip_keys(ps_s, "s", 0, 3, vcopy)
+        scores(0)
+        for c in range(1, 4):
+            flip_queries(ps_p, "p", 0, c, scopy)
+
+        bias_from_mask(nc.gpsimd, 1, 0, L)
+        regroup_v(0)
+        for i in range(2, 7):
+            bias_from_mask(nc.gpsimd, i, 0, L)
+
+        later = {}
+        for c in range(4):
+            later[3 + c] = ("k", c)
+            later[7 + c] = ("q", c)
+
+        for s in range(NU + 2):
+            if s < NU:
+                mask_and_min(s)
+            if s + 1 < NU:
+                scores(s + 1)
+            if 1 <= s <= NU:
+                flip_e(s - 1)
+            if s < NU:
+                exponent(s)
+            if 1 <= s <= NU:
+                group_e(s - 1)
+            if s == 1:
+                quantise_v(0)
+            if s == 2:
+                regroup_v(1)
+                for i in range(7, NT):
+                    bias_from_mask(nc.gpsimd, i, 0, L)
+            if s == 12:
+                quantise_v(1)
+            if s >= 2:
+                quantise_e(s - 2)
+                weighted_sum(s - 2)
+            if s in later:
+                kind, c = later[s]
+                if kind == "k":
+                    flip_keys(ps_p, "p", 1, c, scopy)
+                else:
+                    flip_queries(ps_p, "p", 1, c, scopy)

@@ -23,6 +23,7 @@ CH = 512
 NCH = L // CH
 SCALE = D ** -0.5
 BIG = 1.0e30
+VB = 3
 
 FLOPS = 2 * H * L * L * (2 * D + DV)
 
@@ -33,14 +34,15 @@ def tile_attention_kernel(tc, q, k, v, pe_q, pe_k, mask, out):
         keep = ctx.enter_context(tc.tile_pool(name="keep", bufs=1))
         wpool = ctx.enter_context(tc.tile_pool(name="wpool", bufs=3))
         epool = ctx.enter_context(tc.tile_pool(name="epool", bufs=3))
-        gpool = ctx.enter_context(tc.tile_pool(name="gpool", bufs=2))
+        gpool = ctx.enter_context(tc.tile_pool(name="gpool", bufs=1))
         cpool = ctx.enter_context(tc.tile_pool(name="cpool", bufs=2))
         opool = ctx.enter_context(tc.tile_pool(name="opool", bufs=3))
-        small = ctx.enter_context(tc.tile_pool(name="small", bufs=6))
-        ps_s = ctx.enter_context(tc.psum_pool(name="ps_s", bufs=4))
+        small = ctx.enter_context(tc.tile_pool(name="small", bufs=8))
+        ppool = ctx.enter_context(tc.tile_pool(name="ppool", bufs=4))
+        ps_s = ctx.enter_context(tc.psum_pool(name="ps_s", bufs=3))
+        ps_m = ctx.enter_context(tc.psum_pool(name="ps_m", bufs=2))
         ps_x = ctx.enter_context(tc.psum_pool(name="ps_x", bufs=2))
         ps_o = ctx.enter_context(tc.psum_pool(name="ps_o", bufs=1))
-        ps_p = ctx.enter_context(tc.psum_pool(name="ps_p", bufs=1))
 
         ident = keep.tile([P, P], BF16, name="ident")
         make_identity(nc, ident[:])
@@ -132,36 +134,69 @@ def tile_attention_kernel(tc, q, k, v, pe_q, pe_k, mask, out):
 
         st = {}
 
+        def pe_masked(u):
+            return u < 4 or u >= 12
+
+        def by_gpsimd(u):
+            return u >= 8
+
         def scores(u):
             h, i = divmod(u, NT)
             banks = []
             for j in range(NCH):
-                s = ps_s.tile([P, CH], F32, tag="s", name="s")
+                if j < VB:
+                    s = ps_s.tile([P, CH], F32, tag="s", name="s")
+                else:
+                    s = ps_m.tile([P, CH], F32, tag="m", name="sm")
+                extra = j >= VB and pe_masked(u)
                 cols = slice(CH * j, CH * (j + 1))
                 nc.tensor.matmul(s[:], lhsT=qq[h][:, 0, i, :], rhs=kk[h][:, 0, cols], start=True, stop=False)
-                nc.tensor.matmul(s[:], lhsT=qq[h][:, 1, i, :], rhs=kk[h][:, 1, cols], start=False, stop=True)
+                nc.tensor.matmul(s[:], lhsT=qq[h][:, 1, i, :], rhs=kk[h][:, 1, cols], start=False, stop=not extra)
+                if extra:
+                    nc.tensor.matmul(s[:], lhsT=ident[:], rhs=mb[i][:, cols], start=False, stop=True)
                 banks.append(s)
             st[("s", u)] = banks
 
-        def mask_and_min(u):
+        def mask(u):
             i = u % NT
             w = wpool.tile([P, L], F32, tag="w", name="w")
-            for j in range(NCH):
+            for j in range(VB if pe_masked(u) else NCH):
                 cols = slice(CH * j, CH * (j + 1))
                 nc.vector.scalar_tensor_tensor(
-                    out=w[:, cols], in0=st[("s", u)][j][:], scalar=-SCALE, in1=mb[i][:, cols],
+                    out=w[:, cols], in0=st[("s", u)][j][:], scalar=SCALE, in1=mb[i][:, cols],
                     op0=ALU.mult, op1=ALU.add,
                 )
-            wmin = small.tile([P, 1], F32, tag="wmin", name="wmin")
-            nc.vector.tensor_reduce(out=wmin[:], in_=w[:], axis=AX.X, op=ALU.min)
             st[("w", u)] = w
+
+        def row_min(u):
+            w = st[("w", u)]
+            wmin = small.tile([P, 1], F32, tag="wmin", name="wmin")
+            if pe_masked(u):
+                vmin = small.tile([P, 1], F32, tag="vmin", name="vmin")
+                pmin = small.tile([P, 1], F32, tag="pmin", name="pmin")
+                nc.vector.tensor_reduce(out=pmin[:], in_=st[("s", u)][VB][:], axis=AX.X, op=ALU.min)
+                nc.vector.tensor_reduce(out=vmin[:], in_=w[:, 0:VB * CH], axis=AX.X, op=ALU.min)
+                nc.vector.tensor_scalar(
+                    out=wmin[:], in0=pmin[:], scalar1=SCALE, scalar2=vmin[:], op0=ALU.mult, op1=ALU.min,
+                )
+            else:
+                nc.vector.tensor_reduce(out=wmin[:], in_=w[:], axis=AX.X, op=ALU.min)
             st[("wmin", u)] = wmin
 
         def exponent(u):
             e = epool.tile([P, L], BF16, tag="e", name="e")
             rs = small.tile([P, 1], F32, tag="rs", name="rs")
+            wmin = st[("wmin", u)]
+            if pe_masked(u):
+                rs2 = small.tile([P, 1], F32, tag="rs2", name="rs2")
+                nc.scalar.activation(
+                    out=e[:, VB * CH:L], in_=st[("s", u)][VB][:], func=ACT.Exp, bias=wmin[:], scale=-SCALE,
+                    accum_out=rs2[:],
+                )
+                st[("rs2", u)] = rs2
+            hi = VB * CH if pe_masked(u) else L
             nc.scalar.activation(
-                out=e[:], in_=st[("w", u)][:], func=ACT.Exp, bias=st[("wmin", u)][:], scale=-1.0,
+                out=e[:, 0:hi], in_=st[("w", u)][:, 0:hi], func=ACT.Exp, bias=wmin[:], scale=-1.0,
                 accum_out=rs[:],
             )
             st[("e", u)] = e
@@ -181,10 +216,20 @@ def tile_attention_kernel(tc, q, k, v, pe_q, pe_k, mask, out):
         def group_e(u):
             gr = gpool.tile([P, NCH, P, 4], BF16, tag="gr", name="gr", align_bytes=64)
             for b in range(2):
-                nc.scalar.copy(
-                    out=gr[:, 2 * b:2 * b + 2, :, :],
-                    in_=st[("xt", u)][b][:].rearrange("p (g t) r -> p g r t", t=4),
-                )
+                xt = st[("xt", u)][b]
+                if by_gpsimd(u):
+                    pl = ppool.tile([P, 8, P], BF16, tag="pl", name="pl")
+                    nc.scalar.copy(out=pl[:], in_=xt[:])
+                    nc.gpsimd.tensor_scalar(
+                        out=gr[:, 2 * b:2 * b + 2, :, :],
+                        in0=pl[:].rearrange("p (g t) r -> p g r t", t=4),
+                        scalar1=1.0, scalar2=0.0, op0=ALU.mult, op1=ALU.add,
+                    )
+                else:
+                    nc.scalar.copy(
+                        out=gr[:, 2 * b:2 * b + 2, :, :],
+                        in_=xt[:].rearrange("p (g t) r -> p g r t", t=4),
+                    )
             st[("gr", u)] = gr
 
         def quantise_e(u):
@@ -195,13 +240,16 @@ def tile_attention_kernel(tc, q, k, v, pe_q, pe_k, mask, out):
                 in_=st[("gr", u)][:].rearrange("p g r t -> p (g r t)"),
             )
             rinv = small.tile([P, 1], F32, tag="rinv", name="rinv")
-            nc.vector.reciprocal(rinv[:], st[("rs", u)][:])
+            rs = st[("rs", u)]
+            if pe_masked(u):
+                nc.vector.tensor_tensor(out=rs[:], in0=rs[:], in1=st[("rs2", u)][:], op=ALU.add)
+            nc.vector.reciprocal(rinv[:], rs[:])
             st[("codes", u)] = codes
             st[("scl", u)] = scl
             st[("rinv", u)] = rinv
 
         def weighted_sum(u):
-            h, i = divmod(u, NT)
+            h = u // NT
             o = ps_o.tile([P, DV], F32, tag="o", name="o")
             for g in range(NCH):
                 nc.tensor.matmul_mx(
@@ -212,22 +260,33 @@ def tile_attention_kernel(tc, q, k, v, pe_q, pe_k, mask, out):
                     rhs_scale=vscl[h][:, DV * g:DV * (g + 1)],
                     start=(g == 0), stop=(g == NCH - 1),
                 )
+            st[("o", u)] = o
+
+        def finish(u):
+            h, i = divmod(u, NT)
             res = opool.tile([P, DV], F32, tag="res", name="res")
-            nc.scalar.activation(out=res[:], in_=o[:], func=ACT.Copy, scale=st[("rinv", u)][:])
+            nc.scalar.activation(out=res[:], in_=st[("o", u)][:], func=ACT.Copy, scale=st[("rinv", u)][:])
             nc.sync.dma_start(out=out[0, h].rearrange("(p t) n -> t p n", t=NT)[i], in_=res[:])
 
         vcopy = nc.vector.tensor_copy
         scopy = nc.scalar.copy
-        flip_queries(ps_x, "xt", 0, 0, vcopy)
+
+        def vneg(out, in_):
+            nc.vector.tensor_scalar_mul(out=out, in0=in_, scalar1=-1.0)
+
+        def sneg(out, in_):
+            nc.scalar.mul(out=out, in_=in_, mul=-1.0)
+
+        flip_queries(ps_x, "xt", 0, 0, vneg)
         flip_keys(ps_s, "s", 0, 0, scopy)
         for j in range(NCH):
             bias_from_mask(nc.vector, 0, CH * j, CH * (j + 1))
         flip_keys(ps_s, "s", 0, 1, vcopy)
         flip_keys(ps_s, "s", 0, 2, scopy)
-        flip_keys(ps_s, "s", 0, 3, vcopy)
+        flip_keys(ps_m, "m", 0, 3, vcopy)
         scores(0)
         for c in range(1, 4):
-            flip_queries(ps_p, "p", 0, c, scopy)
+            flip_queries(ps_x, "xt", 0, c, sneg)
 
         bias_from_mask(nc.gpsimd, 1, 0, L)
         regroup_v(0)
@@ -239,9 +298,14 @@ def tile_attention_kernel(tc, q, k, v, pe_q, pe_k, mask, out):
             later[3 + c] = ("k", c)
             later[7 + c] = ("q", c)
 
-        for s in range(NU + 2):
+        for s in range(NU + 3):
             if s < NU:
-                mask_and_min(s)
+                mask(s)
+            if 3 <= s and by_gpsimd(s - 3):
+                quantise_e(s - 3)
+                weighted_sum(s - 3)
+            if s < NU:
+                row_min(s)
             if s + 1 < NU:
                 scores(s + 1)
             if 1 <= s <= NU:
@@ -258,12 +322,15 @@ def tile_attention_kernel(tc, q, k, v, pe_q, pe_k, mask, out):
                     bias_from_mask(nc.gpsimd, i, 0, L)
             if s == 12:
                 quantise_v(1)
-            if s >= 2:
+            if 2 <= s and s - 2 < NU and not by_gpsimd(s - 2):
                 quantise_e(s - 2)
                 weighted_sum(s - 2)
+                finish(s - 2)
+            if 3 <= s and by_gpsimd(s - 3):
+                finish(s - 3)
             if s in later:
                 kind, c = later[s]
                 if kind == "k":
-                    flip_keys(ps_p, "p", 1, c, scopy)
+                    flip_keys(ps_m, "m", 1, c, scopy)
                 else:
-                    flip_queries(ps_p, "p", 1, c, scopy)
+                    flip_queries(ps_m, "m", 1, c, sneg)

@@ -34,7 +34,7 @@ def tile_attention_kernel(tc, q, k, v, pe_q, pe_k, mask, out):
         keep = ctx.enter_context(tc.tile_pool(name="keep", bufs=1))
         wpool = ctx.enter_context(tc.tile_pool(name="wpool", bufs=3))
         epool = ctx.enter_context(tc.tile_pool(name="epool", bufs=3))
-        gpool = ctx.enter_context(tc.tile_pool(name="gpool", bufs=1))
+        gpool = ctx.enter_context(tc.tile_pool(name="gpool", bufs=2))
         cpool = ctx.enter_context(tc.tile_pool(name="cpool", bufs=2))
         opool = ctx.enter_context(tc.tile_pool(name="opool", bufs=3))
         small = ctx.enter_context(tc.tile_pool(name="small", bufs=8))
@@ -138,7 +138,7 @@ def tile_attention_kernel(tc, q, k, v, pe_q, pe_k, mask, out):
             return u < 4 or u >= 12
 
         def by_gpsimd(u):
-            return u >= 8
+            return False
 
         def scores(u):
             h, i = divmod(u, NT)

@@ -23,7 +23,6 @@ CH = 512
 NCH = L // CH
 SCALE = D ** -0.5
 BIG = 1.0e30
-VB = 3
 
 FLOPS = 2 * H * L * L * (2 * D + DV)
 
@@ -32,20 +31,21 @@ def tile_attention_kernel(tc, q, k, v, pe_q, pe_k, mask, out):
     nc = tc.nc
     with ExitStack() as ctx:
         keep = ctx.enter_context(tc.tile_pool(name="keep", bufs=1))
-        wpool = ctx.enter_context(tc.tile_pool(name="wpool", bufs=3))
+        wpool = ctx.enter_context(tc.tile_pool(name="wpool", bufs=4))
         epool = ctx.enter_context(tc.tile_pool(name="epool", bufs=3))
         gpool = ctx.enter_context(tc.tile_pool(name="gpool", bufs=2))
         cpool = ctx.enter_context(tc.tile_pool(name="cpool", bufs=2))
         opool = ctx.enter_context(tc.tile_pool(name="opool", bufs=3))
-        small = ctx.enter_context(tc.tile_pool(name="small", bufs=8))
-        ppool = ctx.enter_context(tc.tile_pool(name="ppool", bufs=4))
-        ps_s = ctx.enter_context(tc.psum_pool(name="ps_s", bufs=3))
-        ps_m = ctx.enter_context(tc.psum_pool(name="ps_m", bufs=2))
+        small = ctx.enter_context(tc.tile_pool(name="small", bufs=6))
+        ps_s = ctx.enter_context(tc.psum_pool(name="ps_s", bufs=4))
         ps_x = ctx.enter_context(tc.psum_pool(name="ps_x", bufs=2))
         ps_o = ctx.enter_context(tc.psum_pool(name="ps_o", bufs=1))
+        ps_p = ctx.enter_context(tc.psum_pool(name="ps_p", bufs=1))
 
         ident = keep.tile([P, P], BF16, name="ident")
         make_identity(nc, ident[:])
+        negident = keep.tile([P, P], BF16, name="negident")
+        nc.vector.tensor_scalar_mul(out=negident[:], in0=ident[:], scalar1=-1.0)
 
         raw = {}
         for h in range(H):
@@ -64,8 +64,11 @@ def tile_attention_kernel(tc, q, k, v, pe_q, pe_k, mask, out):
                 in_=src[0, h].rearrange("(t p) d -> p t d", p=P)[:, lo:hi, :],
             )
 
-        def load_queries(nm, src, h):
-            nc.sync.dma_start(out=raw[(nm, h)][:], in_=src[0, h].rearrange("(p t) d -> p t d", t=NT))
+        def load_queries(nm, src, h, lo, hi):
+            nc.sync.dma_start(
+                out=raw[(nm, h)][:, lo:hi, :],
+                in_=src[0, h].rearrange("(p t) d -> p t d", t=NT)[:, lo:hi, :],
+            )
 
         def load_mask(i):
             nc.sync.dma_start(out=mb[i][:], in_=mask[0].rearrange("(p t) c -> t p c", t=NT)[i])
@@ -73,26 +76,34 @@ def tile_attention_kernel(tc, q, k, v, pe_q, pe_k, mask, out):
         def load_v(h):
             nc.sync.dma_start(out=vraw[h][:], in_=v[0, h].rearrange("(c p) n -> p c n", p=P))
 
-        load_keys("k", k, 0, 0, 8)
-        load_keys("pk", pe_k, 0, 0, 8)
-        load_queries("q", q, 0)
-        load_queries("pq", pe_q, 0)
+        load_keys("k", k, 0, 0, 4)
+        load_keys("pk", pe_k, 0, 0, 4)
+        load_queries("q", q, 0, 0, 4)
+        load_queries("pq", pe_q, 0, 0, 4)
         load_mask(0)
+        load_keys("k", k, 0, 4, 8)
+        load_keys("pk", pe_k, 0, 4, 8)
         load_keys("k", k, 0, 8, NT)
         load_keys("pk", pe_k, 0, 8, NT)
         load_mask(1)
+        load_queries("q", q, 0, 4, NT)
+        load_queries("pq", pe_q, 0, 4, NT)
         load_v(0)
         load_mask(2)
         load_mask(3)
         load_keys("k", k, 1, 0, NT)
         load_keys("pk", pe_k, 1, 0, NT)
         load_mask(4)
-        load_queries("q", q, 1)
-        load_queries("pq", pe_q, 1)
+        load_queries("q", q, 1, 0, NT)
+        load_queries("pq", pe_q, 1, 0, NT)
         load_mask(5)
         load_v(1)
         for i in range(6, NT):
             load_mask(i)
+
+        warm = small.tile([P, 1], F32, tag="warm", name="warm", bufs=1)
+        nc.vector.memset(warm[:], 0.0)
+        nc.scalar.activation(out=warm[:], in_=warm[:], func=ACT.Exp)
 
         def bias_from_mask(eng, i, lo, hi):
             eng.tensor_scalar(
@@ -135,72 +146,62 @@ def tile_attention_kernel(tc, q, k, v, pe_q, pe_k, mask, out):
         st = {}
 
         def pe_masked(u):
-            return u < 4 or u >= 12
-
-        def by_gpsimd(u):
-            return False
+            return u % 4 != 3
 
         def scores(u):
             h, i = divmod(u, NT)
             banks = []
             for j in range(NCH):
-                if j < VB:
-                    s = ps_s.tile([P, CH], F32, tag="s", name="s")
-                else:
-                    s = ps_m.tile([P, CH], F32, tag="m", name="sm")
-                extra = j >= VB and pe_masked(u)
+                s = ps_s.tile([P, CH], F32, tag="s", name="s")
                 cols = slice(CH * j, CH * (j + 1))
                 nc.tensor.matmul(s[:], lhsT=qq[h][:, 0, i, :], rhs=kk[h][:, 0, cols], start=True, stop=False)
+                extra = j == NCH - 1 and pe_masked(u)
                 nc.tensor.matmul(s[:], lhsT=qq[h][:, 1, i, :], rhs=kk[h][:, 1, cols], start=False, stop=not extra)
                 if extra:
-                    nc.tensor.matmul(s[:], lhsT=ident[:], rhs=mb[i][:, cols], start=False, stop=True)
+                    nc.tensor.matmul(s[:], lhsT=negident[:], rhs=mb[i][:, cols], start=False, stop=True)
                 banks.append(s)
             st[("s", u)] = banks
 
-        def mask(u):
+        def mask_and_min(u):
             i = u % NT
             w = wpool.tile([P, L], F32, tag="w", name="w")
-            for j in range(VB if pe_masked(u) else NCH):
+            nv = NCH - 1 if pe_masked(u) else NCH
+            for j in range(nv):
                 cols = slice(CH * j, CH * (j + 1))
                 nc.vector.scalar_tensor_tensor(
-                    out=w[:, cols], in0=st[("s", u)][j][:], scalar=SCALE, in1=mb[i][:, cols],
+                    out=w[:, cols], in0=st[("s", u)][j][:], scalar=-SCALE, in1=mb[i][:, cols],
                     op0=ALU.mult, op1=ALU.add,
                 )
-            st[("w", u)] = w
-
-        def row_min(u):
-            w = st[("w", u)]
             wmin = small.tile([P, 1], F32, tag="wmin", name="wmin")
             if pe_masked(u):
                 vmin = small.tile([P, 1], F32, tag="vmin", name="vmin")
-                pmin = small.tile([P, 1], F32, tag="pmin", name="pmin")
-                nc.vector.tensor_reduce(out=pmin[:], in_=st[("s", u)][VB][:], axis=AX.X, op=ALU.min)
-                nc.vector.tensor_reduce(out=vmin[:], in_=w[:, 0:VB * CH], axis=AX.X, op=ALU.min)
+                nc.vector.tensor_reduce(out=vmin[:], in_=w[:, 0:CH * nv], axis=AX.X, op=ALU.min)
                 nc.vector.tensor_scalar(
-                    out=wmin[:], in0=pmin[:], scalar1=SCALE, scalar2=vmin[:], op0=ALU.mult, op1=ALU.min,
+                    out=w[:, CH * nv:L], in0=st[("s", u)][nv][:], scalar1=-SCALE, scalar2=vmin[:],
+                    op0=ALU.mult, op1=ALU.min, accum_out=wmin[:],
                 )
             else:
                 nc.vector.tensor_reduce(out=wmin[:], in_=w[:], axis=AX.X, op=ALU.min)
+            st[("w", u)] = w
             st[("wmin", u)] = wmin
+
+        def pieces(u):
+            return 2 if u == NU - 1 else 1
 
         def exponent(u):
             e = epool.tile([P, L], BF16, tag="e", name="e")
-            rs = small.tile([P, 1], F32, tag="rs", name="rs")
-            wmin = st[("wmin", u)]
-            if pe_masked(u):
-                rs2 = small.tile([P, 1], F32, tag="rs2", name="rs2")
+            width = L // pieces(u)
+            sums = []
+            for a in range(pieces(u)):
+                rs = small.tile([P, 1], F32, tag="rs", name="rs")
+                cols = slice(a * width, (a + 1) * width)
                 nc.scalar.activation(
-                    out=e[:, VB * CH:L], in_=st[("s", u)][VB][:], func=ACT.Exp, bias=wmin[:], scale=-SCALE,
-                    accum_out=rs2[:],
+                    out=e[:, cols], in_=st[("w", u)][:, cols], func=ACT.Exp, bias=st[("wmin", u)][:], scale=-1.0,
+                    accum_out=rs[:],
                 )
-                st[("rs2", u)] = rs2
-            hi = VB * CH if pe_masked(u) else L
-            nc.scalar.activation(
-                out=e[:, 0:hi], in_=st[("w", u)][:, 0:hi], func=ACT.Exp, bias=wmin[:], scale=-1.0,
-                accum_out=rs[:],
-            )
+                sums.append(rs)
             st[("e", u)] = e
-            st[("rs", u)] = rs
+            st[("rs", u)] = sums
 
         def flip_e(u):
             e = st[("e", u)]
@@ -216,40 +217,34 @@ def tile_attention_kernel(tc, q, k, v, pe_q, pe_k, mask, out):
         def group_e(u):
             gr = gpool.tile([P, NCH, P, 4], BF16, tag="gr", name="gr", align_bytes=64)
             for b in range(2):
-                xt = st[("xt", u)][b]
-                if by_gpsimd(u):
-                    pl = ppool.tile([P, 8, P], BF16, tag="pl", name="pl")
-                    nc.scalar.copy(out=pl[:], in_=xt[:])
-                    nc.gpsimd.tensor_scalar(
-                        out=gr[:, 2 * b:2 * b + 2, :, :],
-                        in0=pl[:].rearrange("p (g t) r -> p g r t", t=4),
-                        scalar1=1.0, scalar2=0.0, op0=ALU.mult, op1=ALU.add,
-                    )
-                else:
-                    nc.scalar.copy(
-                        out=gr[:, 2 * b:2 * b + 2, :, :],
-                        in_=xt[:].rearrange("p (g t) r -> p g r t", t=4),
-                    )
+                copy = nc.vector.tensor_copy if (u >= NU - 2 and b == 0) else nc.scalar.copy
+                copy(
+                    out=gr[:, 2 * b:2 * b + 2, :, :],
+                    in_=st[("xt", u)][b][:].rearrange("p (g t) r -> p g r t", t=4),
+                )
             st[("gr", u)] = gr
 
         def quantise_e(u):
             codes = cpool.tile([P, NCH * P], U32, tag="codes", name="codes", align_bytes=64)
             scl = cpool.tile([P, NCH * P], U8, tag="scl", name="scl", align_bytes=64)
-            nc.vector.quantize_mx(
-                out=codes[:].bitcast(FP8X4), scales=scl[:],
-                in_=st[("gr", u)][:].rearrange("p g r t -> p (g r t)"),
-            )
+            n = pieces(u)
+            for a in range(n):
+                words = slice(a * NCH * P // n, (a + 1) * NCH * P // n)
+                nc.vector.quantize_mx(
+                    out=codes[:, words].bitcast(FP8X4), scales=scl[:, words],
+                    in_=st[("gr", u)][:, a * NCH // n:(a + 1) * NCH // n, :, :].rearrange("p g r t -> p (g r t)"),
+                )
             rinv = small.tile([P, 1], F32, tag="rinv", name="rinv")
-            rs = st[("rs", u)]
-            if pe_masked(u):
-                nc.vector.tensor_tensor(out=rs[:], in0=rs[:], in1=st[("rs2", u)][:], op=ALU.add)
-            nc.vector.reciprocal(rinv[:], rs[:])
+            sums = st[("rs", u)]
+            if n == 2:
+                nc.vector.tensor_tensor(out=sums[0][:], in0=sums[0][:], in1=sums[1][:], op=ALU.add)
+            nc.vector.reciprocal(rinv[:], sums[0][:])
             st[("codes", u)] = codes
             st[("scl", u)] = scl
             st[("rinv", u)] = rinv
 
         def weighted_sum(u):
-            h = u // NT
+            h, i = divmod(u, NT)
             o = ps_o.tile([P, DV], F32, tag="o", name="o")
             for g in range(NCH):
                 nc.tensor.matmul_mx(
@@ -260,33 +255,25 @@ def tile_attention_kernel(tc, q, k, v, pe_q, pe_k, mask, out):
                     rhs_scale=vscl[h][:, DV * g:DV * (g + 1)],
                     start=(g == 0), stop=(g == NCH - 1),
                 )
-            st[("o", u)] = o
-
-        def finish(u):
-            h, i = divmod(u, NT)
             res = opool.tile([P, DV], F32, tag="res", name="res")
-            nc.scalar.activation(out=res[:], in_=st[("o", u)][:], func=ACT.Copy, scale=st[("rinv", u)][:])
+            if u >= NU - 3:
+                nc.vector.tensor_scalar_mul(out=res[:], in0=o[:], scalar1=st[("rinv", u)][:])
+            else:
+                nc.scalar.activation(out=res[:], in_=o[:], func=ACT.Copy, scale=st[("rinv", u)][:])
             nc.sync.dma_start(out=out[0, h].rearrange("(p t) n -> t p n", t=NT)[i], in_=res[:])
 
         vcopy = nc.vector.tensor_copy
         scopy = nc.scalar.copy
-
-        def vneg(out, in_):
-            nc.vector.tensor_scalar_mul(out=out, in0=in_, scalar1=-1.0)
-
-        def sneg(out, in_):
-            nc.scalar.mul(out=out, in_=in_, mul=-1.0)
-
-        flip_queries(ps_x, "xt", 0, 0, vneg)
+        flip_queries(ps_x, "xt", 0, 0, vcopy)
         flip_keys(ps_s, "s", 0, 0, scopy)
         for j in range(NCH):
             bias_from_mask(nc.vector, 0, CH * j, CH * (j + 1))
         flip_keys(ps_s, "s", 0, 1, vcopy)
         flip_keys(ps_s, "s", 0, 2, scopy)
-        flip_keys(ps_m, "m", 0, 3, vcopy)
+        flip_keys(ps_s, "s", 0, 3, vcopy)
         scores(0)
         for c in range(1, 4):
-            flip_queries(ps_x, "xt", 0, c, sneg)
+            flip_queries(ps_p, "p", 0, c, scopy)
 
         bias_from_mask(nc.gpsimd, 1, 0, L)
         regroup_v(0)
@@ -298,14 +285,9 @@ def tile_attention_kernel(tc, q, k, v, pe_q, pe_k, mask, out):
             later[3 + c] = ("k", c)
             later[7 + c] = ("q", c)
 
-        for s in range(NU + 3):
+        for s in range(NU + 2):
             if s < NU:
-                mask(s)
-            if 3 <= s and by_gpsimd(s - 3):
-                quantise_e(s - 3)
-                weighted_sum(s - 3)
-            if s < NU:
-                row_min(s)
+                mask_and_min(s)
             if s + 1 < NU:
                 scores(s + 1)
             if 1 <= s <= NU:
@@ -322,15 +304,12 @@ def tile_attention_kernel(tc, q, k, v, pe_q, pe_k, mask, out):
                     bias_from_mask(nc.gpsimd, i, 0, L)
             if s == 12:
                 quantise_v(1)
-            if 2 <= s and s - 2 < NU and not by_gpsimd(s - 2):
+            if s >= 2:
                 quantise_e(s - 2)
                 weighted_sum(s - 2)
-                finish(s - 2)
-            if 3 <= s and by_gpsimd(s - 3):
-                finish(s - 3)
             if s in later:
                 kind, c = later[s]
                 if kind == "k":
-                    flip_keys(ps_m, "m", 1, c, scopy)
+                    flip_keys(ps_p, "p", 1, c, scopy if c % 2 else vcopy)
                 else:
-                    flip_queries(ps_m, "m", 1, c, sneg)
+                    flip_queries(ps_p, "p", 1, c, scopy if c % 2 else vcopy)

@@ -256,7 +256,7 @@ def tile_attention_kernel(tc, q, k, v, pe_q, pe_k, mask, out):
                     start=(g == 0), stop=(g == NCH - 1),
                 )
             res = opool.tile([P, DV], F32, tag="res", name="res")
-            if u >= NU - 3:
+            if u >= NU - 3 or pe_masked(u):
                 nc.vector.tensor_scalar_mul(out=res[:], in0=o[:], scalar1=st[("rinv", u)][:])
             else:
                 nc.scalar.activation(out=res[:], in_=o[:], func=ACT.Copy, scale=st[("rinv", u)][:])

@@ -85,11 +85,11 @@ def tile_attention_kernel(tc, q, k, v, pe_q, pe_k, mask, out):
         load_keys("pk", pe_k, 0, 4, 8)
         load_keys("k", k, 0, 8, NT)
         load_keys("pk", pe_k, 0, 8, NT)
+        load_v(0)
         load_mask(1)
+        load_mask(2)
         load_queries("q", q, 0, 4, NT)
         load_queries("pq", pe_q, 0, 4, NT)
-        load_v(0)
-        load_mask(2)
         load_mask(3)
         load_keys("k", k, 1, 0, NT)
         load_keys("pk", pe_k, 1, 0, NT)
@@ -101,6 +101,8 @@ def tile_attention_kernel(tc, q, k, v, pe_q, pe_k, mask, out):
         for i in range(6, NT):
             load_mask(i)
 
+        huge = keep.tile([P, 1], F32, name="huge")
+        nc.vector.memset(huge[:], 3.0e38)
         warm = small.tile([P, 1], F32, tag="warm", name="warm", bufs=1)
         nc.vector.memset(warm[:], 0.0)
         nc.scalar.activation(out=warm[:], in_=warm[:], func=ACT.Exp)
@@ -148,10 +150,13 @@ def tile_attention_kernel(tc, q, k, v, pe_q, pe_k, mask, out):
         def pe_masked(u):
             return u % 4 != 3
 
+        def bank_order(u):
+            return (0, 1, 3, 2) if pe_masked(u) else (0, 1, 2, 3)
+
         def scores(u):
             h, i = divmod(u, NT)
-            banks = []
-            for j in range(NCH):
+            banks = {}
+            for j in bank_order(u):
                 s = ps_s.tile([P, CH], F32, tag="s", name="s")
                 cols = slice(CH * j, CH * (j + 1))
                 nc.tensor.matmul(s[:], lhsT=qq[h][:, 0, i, :], rhs=kk[h][:, 0, cols], start=True, stop=False)
@@ -159,29 +164,40 @@ def tile_attention_kernel(tc, q, k, v, pe_q, pe_k, mask, out):
                 nc.tensor.matmul(s[:], lhsT=qq[h][:, 1, i, :], rhs=kk[h][:, 1, cols], start=False, stop=not extra)
                 if extra:
                     nc.tensor.matmul(s[:], lhsT=negident[:], rhs=mb[i][:, cols], start=False, stop=True)
-                banks.append(s)
+                banks[j] = s
             st[("s", u)] = banks
 
         def mask_and_min(u):
             i = u % NT
             w = wpool.tile([P, L], F32, tag="w", name="w")
-            nv = NCH - 1 if pe_masked(u) else NCH
-            for j in range(nv):
+            part = small.tile([P, NCH], F32, tag="part", name="part")
+
+            def leave_psum(j):
                 cols = slice(CH * j, CH * (j + 1))
-                nc.vector.scalar_tensor_tensor(
-                    out=w[:, cols], in0=st[("s", u)][j][:], scalar=-SCALE, in1=mb[i][:, cols],
-                    op0=ALU.mult, op1=ALU.add,
-                )
+                if j == NCH - 1 and pe_masked(u):
+                    nc.vector.tensor_scalar(
+                        out=w[:, cols], in0=st[("s", u)][j][:], scalar1=-SCALE, scalar2=huge[:],
+                        op0=ALU.mult, op1=ALU.min, accum_out=part[:, j:j + 1],
+                    )
+                else:
+                    nc.vector.scalar_tensor_tensor(
+                        out=w[:, cols], in0=st[("s", u)][j][:], scalar=-SCALE, in1=mb[i][:, cols],
+                        op0=ALU.mult, op1=ALU.add,
+                    )
+
+            def bank_min(j):
+                if not (j == NCH - 1 and pe_masked(u)):
+                    cols = slice(CH * j, CH * (j + 1))
+                    nc.vector.tensor_reduce(out=part[:, j:j + 1], in_=w[:, cols], axis=AX.X, op=ALU.min)
+
+            order = bank_order(u)
+            leave_psum(order[0])
+            for n in range(1, NCH):
+                leave_psum(order[n])
+                bank_min(order[n - 1])
+            bank_min(order[NCH - 1])
             wmin = small.tile([P, 1], F32, tag="wmin", name="wmin")
-            if pe_masked(u):
-                vmin = small.tile([P, 1], F32, tag="vmin", name="vmin")
-                nc.vector.tensor_reduce(out=vmin[:], in_=w[:, 0:CH * nv], axis=AX.X, op=ALU.min)
-                nc.vector.tensor_scalar(
-                    out=w[:, CH * nv:L], in0=st[("s", u)][nv][:], scalar1=-SCALE, scalar2=vmin[:],
-                    op0=ALU.mult, op1=ALU.min, accum_out=wmin[:],
-                )
-            else:
-                nc.vector.tensor_reduce(out=wmin[:], in_=w[:], axis=AX.X, op=ALU.min)
+            nc.vector.tensor_reduce(out=wmin[:], in_=part[:], axis=AX.X, op=ALU.min)
             st[("w", u)] = w
             st[("wmin", u)] = wmin
 
@@ -256,7 +272,7 @@ def tile_attention_kernel(tc, q, k, v, pe_q, pe_k, mask, out):
                     start=(g == 0), stop=(g == NCH - 1),
                 )
             res = opool.tile([P, DV], F32, tag="res", name="res")
-            if u >= NU - 3 or pe_masked(u):
+            if u >= NU - 3:
                 nc.vector.tensor_scalar_mul(out=res[:], in0=o[:], scalar1=st[("rinv", u)][:])
             else:
                 nc.scalar.activation(out=res[:], in_=o[:], func=ACT.Copy, scale=st[("rinv", u)][:])
@@ -275,9 +291,8 @@ def tile_attention_kernel(tc, q, k, v, pe_q, pe_k, mask, out):
         for c in range(1, 4):
             flip_queries(ps_p, "p", 0, c, scopy)
 
-        bias_from_mask(nc.gpsimd, 1, 0, L)
         regroup_v(0)
-        for i in range(2, 7):
+        for i in range(3, 7):
             bias_from_mask(nc.gpsimd, i, 0, L)
 
         later = {}
@@ -288,6 +303,8 @@ def tile_attention_kernel(tc, q, k, v, pe_q, pe_k, mask, out):
         for s in range(NU + 2):
             if s < NU:
                 mask_and_min(s)
+            if s < 2:
+                bias_from_mask(nc.vector, s + 1, 0, L)
             if s + 1 < NU:
                 scores(s + 1)
             if 1 <= s <= NU:
@@ -296,9 +313,8 @@ def tile_attention_kernel(tc, q, k, v, pe_q, pe_k, mask, out):
                 exponent(s)
             if 1 <= s <= NU:
                 group_e(s - 1)
-            if s == 1:
-                quantise_v(0)
             if s == 2:
+                quantise_v(0)
                 regroup_v(1)
                 for i in range(7, NT):
                     bias_from_mask(nc.gpsimd, i, 0, L)

@@ -85,11 +85,11 @@ def tile_attention_kernel(tc, q, k, v, pe_q, pe_k, mask, out):
         load_keys("pk", pe_k, 0, 4, 8)
         load_keys("k", k, 0, 8, NT)
         load_keys("pk", pe_k, 0, 8, NT)
-        load_v(0)
         load_mask(1)
-        load_mask(2)
         load_queries("q", q, 0, 4, NT)
         load_queries("pq", pe_q, 0, 4, NT)
+        load_v(0)
+        load_mask(2)
         load_mask(3)
         load_keys("k", k, 1, 0, NT)
         load_keys("pk", pe_k, 1, 0, NT)
@@ -101,8 +101,6 @@ def tile_attention_kernel(tc, q, k, v, pe_q, pe_k, mask, out):
         for i in range(6, NT):
             load_mask(i)
 
-        huge = keep.tile([P, 1], F32, name="huge")
-        nc.vector.memset(huge[:], 3.0e38)
         warm = small.tile([P, 1], F32, tag="warm", name="warm", bufs=1)
         nc.vector.memset(warm[:], 0.0)
         nc.scalar.activation(out=warm[:], in_=warm[:], func=ACT.Exp)
@@ -150,13 +148,10 @@ def tile_attention_kernel(tc, q, k, v, pe_q, pe_k, mask, out):
         def pe_masked(u):
             return u % 4 != 3
 
-        def bank_order(u):
-            return (0, 1, 3, 2) if pe_masked(u) else (0, 1, 2, 3)
-
         def scores(u):
             h, i = divmod(u, NT)
-            banks = {}
-            for j in bank_order(u):
+            banks = []
+            for j in range(NCH):
                 s = ps_s.tile([P, CH], F32, tag="s", name="s")
                 cols = slice(CH * j, CH * (j + 1))
                 nc.tensor.matmul(s[:], lhsT=qq[h][:, 0, i, :], rhs=kk[h][:, 0, cols], start=True, stop=False)
@@ -164,40 +159,29 @@ def tile_attention_kernel(tc, q, k, v, pe_q, pe_k, mask, out):
                 nc.tensor.matmul(s[:], lhsT=qq[h][:, 1, i, :], rhs=kk[h][:, 1, cols], start=False, stop=not extra)
                 if extra:
                     nc.tensor.matmul(s[:], lhsT=negident[:], rhs=mb[i][:, cols], start=False, stop=True)
-                banks[j] = s
+                banks.append(s)
             st[("s", u)] = banks
 
         def mask_and_min(u):
             i = u % NT
             w = wpool.tile([P, L], F32, tag="w", name="w")
-            part = small.tile([P, NCH], F32, tag="part", name="part")
-
-            def leave_psum(j):
+            nv = NCH - 1 if pe_masked(u) else NCH
+            for j in range(nv):
                 cols = slice(CH * j, CH * (j + 1))
-                if j == NCH - 1 and pe_masked(u):
-                    nc.vector.tensor_scalar(
-                        out=w[:, cols], in0=st[("s", u)][j][:], scalar1=-SCALE, scalar2=huge[:],
-                        op0=ALU.mult, op1=ALU.min, accum_out=part[:, j:j + 1],
-                    )
-                else:
-                    nc.vector.scalar_tensor_tensor(
-                        out=w[:, cols], in0=st[("s", u)][j][:], scalar=-SCALE, in1=mb[i][:, cols],
-                        op0=ALU.mult, op1=ALU.add,
-                    )
-
-            def bank_min(j):
-                if not (j == NCH - 1 and pe_masked(u)):
-                    cols = slice(CH * j, CH * (j + 1))
-                    nc.vector.tensor_reduce(out=part[:, j:j + 1], in_=w[:, cols], axis=AX.X, op=ALU.min)
-
-            order = bank_order(u)
-            leave_psum(order[0])
-            for n in range(1, NCH):
-                leave_psum(order[n])
-                bank_min(order[n - 1])
-            bank_min(order[NCH - 1])
+                nc.vector.scalar_tensor_tensor(
+                    out=w[:, cols], in0=st[("s", u)][j][:], scalar=-SCALE, in1=mb[i][:, cols],
+                    op0=ALU.mult, op1=ALU.add,
+                )
             wmin = small.tile([P, 1], F32, tag="wmin", name="wmin")
-            nc.vector.tensor_reduce(out=wmin[:], in_=part[:], axis=AX.X, op=ALU.min)
+            if pe_masked(u):
+                vmin = small.tile([P, 1], F32, tag="vmin", name="vmin")
+                nc.vector.tensor_reduce(out=vmin[:], in_=w[:, 0:CH * nv], axis=AX.X, op=ALU.min)
+                nc.vector.tensor_scalar(
+                    out=w[:, CH * nv:L], in0=st[("s", u)][nv][:], scalar1=-SCALE, scalar2=vmin[:],
+                    op0=ALU.mult, op1=ALU.min, accum_out=wmin[:],
+                )
+            else:
+                nc.vector.tensor_reduce(out=wmin[:], in_=w[:], axis=AX.X, op=ALU.min)
             st[("w", u)] = w
             st[("wmin", u)] = wmin
 
@@ -271,8 +255,16 @@ def tile_attention_kernel(tc, q, k, v, pe_q, pe_k, mask, out):
                     rhs_scale=vscl[h][:, DV * g:DV * (g + 1)],
                     start=(g == 0), stop=(g == NCH - 1),
                 )
+            st[("o", u)] = o
+
+        def on_vector(u):
+            return pe_masked(u) and u < NU - 3
+
+        def finish(u):
+            h, i = divmod(u, NT)
+            o = st[("o", u)]
             res = opool.tile([P, DV], F32, tag="res", name="res")
-            if u >= NU - 3:
+            if u >= NU - 3 or on_vector(u):
                 nc.vector.tensor_scalar_mul(out=res[:], in0=o[:], scalar1=st[("rinv", u)][:])
             else:
                 nc.scalar.activation(out=res[:], in_=o[:], func=ACT.Copy, scale=st[("rinv", u)][:])
@@ -291,8 +283,9 @@ def tile_attention_kernel(tc, q, k, v, pe_q, pe_k, mask, out):
         for c in range(1, 4):
             flip_queries(ps_p, "p", 0, c, scopy)
 
+        bias_from_mask(nc.gpsimd, 1, 0, L)
         regroup_v(0)
-        for i in range(3, 7):
+        for i in range(2, 7):
             bias_from_mask(nc.gpsimd, i, 0, L)
 
         later = {}
@@ -303,8 +296,8 @@ def tile_attention_kernel(tc, q, k, v, pe_q, pe_k, mask, out):
         for s in range(NU + 2):
             if s < NU:
                 mask_and_min(s)
-            if s < 2:
-                bias_from_mask(nc.vector, s + 1, 0, L)
+            if s >= 3 and on_vector(s - 3):
+                finish(s - 3)
             if s + 1 < NU:
                 scores(s + 1)
             if 1 <= s <= NU:
@@ -313,8 +306,9 @@ def tile_attention_kernel(tc, q, k, v, pe_q, pe_k, mask, out):
                 exponent(s)
             if 1 <= s <= NU:
                 group_e(s - 1)
-            if s == 2:
+            if s == 1:
                 quantise_v(0)
+            if s == 2:
                 regroup_v(1)
                 for i in range(7, NT):
                     bias_from_mask(nc.gpsimd, i, 0, L)
@@ -323,9 +317,11 @@ def tile_attention_kernel(tc, q, k, v, pe_q, pe_k, mask, out):
             if s >= 2:
                 quantise_e(s - 2)
                 weighted_sum(s - 2)
+                if not on_vector(s - 2):
+                    finish(s - 2)
             if s in later:
                 kind, c = later[s]
                 if kind == "k":
-                    flip_keys(ps_p, "p", 1, c, scopy if c % 2 else vcopy)
+                    flip_keys(ps_p, "p", 1, c, vcopy)
                 else:
-                    flip_queries(ps_p, "p", 1, c, scopy if c % 2 else vcopy)
+                    flip_queries(ps_p, "p", 1, c, vcopy)

from contextlib import ExitStack

import concourse.mybir as mybir
from concourse.masks import make_identity

F32 = mybir.dt.float32
BF16 = mybir.dt.bfloat16
U32 = mybir.dt.uint32
U8 = mybir.dt.uint8
FP8X4 = mybir.dt.float8_e4m3fn_x4
ALU = mybir.AluOpType
ACT = mybir.ActivationFunctionType
AX = mybir.AxisListType

P = 128
H = 2
L = 2048
D = 128
DV = 256
NT = L // P
NU = H * NT
CH = 512
NCH = L // CH
SCALE = D ** -0.5
BIG = 1.0e30

FLOPS = 2 * H * L * L * (2 * D + DV)


def tile_attention_kernel(tc, q, k, v, pe_q, pe_k, mask, out):
    nc = tc.nc
    with ExitStack() as ctx:
        keep = ctx.enter_context(tc.tile_pool(name="keep", bufs=1))
        wpool = ctx.enter_context(tc.tile_pool(name="wpool", bufs=4))
        epool = ctx.enter_context(tc.tile_pool(name="epool", bufs=3))
        gpool = ctx.enter_context(tc.tile_pool(name="gpool", bufs=2))
        cpool = ctx.enter_context(tc.tile_pool(name="cpool", bufs=2))
        opool = ctx.enter_context(tc.tile_pool(name="opool", bufs=3))
        small = ctx.enter_context(tc.tile_pool(name="small", bufs=6))
        ps_s = ctx.enter_context(tc.psum_pool(name="ps_s", bufs=4))
        ps_x = ctx.enter_context(tc.psum_pool(name="ps_x", bufs=2))
        ps_o = ctx.enter_context(tc.psum_pool(name="ps_o", bufs=1))
        ps_p = ctx.enter_context(tc.psum_pool(name="ps_p", bufs=1))

        ident = keep.tile([P, P], BF16, name="ident")
        make_identity(nc, ident[:])
        negident = keep.tile([P, P], BF16, name="negident")
        nc.vector.tensor_scalar_mul(out=negident[:], in0=ident[:], scalar1=-1.0)

        raw = {}
        for h in range(H):
            for nm in ("q", "pq", "k", "pk"):
                raw[(nm, h)] = keep.tile([P, NT, D], BF16, name="raw_%s%d" % (nm, h))
        qq = [keep.tile([P, 2, NT, P], BF16, name="qq%d" % h) for h in range(H)]
        kk = [keep.tile([P, 2, L], BF16, name="kk%d" % h) for h in range(H)]
        mb = [keep.tile([P, L], BF16, name="mb%d" % i) for i in range(NT)]
        vraw = [keep.tile([P, NT, DV], BF16, name="vraw%d" % h) for h in range(H)]
        vcodes = [keep.tile([P, NCH * DV], U32, name="vcodes%d" % h, align_bytes=64) for h in range(H)]
        vscl = [keep.tile([P, NCH * DV], U8, name="vscl%d" % h, align_bytes=64) for h in range(H)]

        def load_keys(nm, src, h, lo, hi):
            nc.sync.dma_start(
                out=raw[(nm, h)][:, lo:hi, :],
                in_=src[0, h].rearrange("(t p) d -> p t d", p=P)[:, lo:hi, :],
            )

        def load_queries(nm, src, h, lo, hi):
            nc.sync.dma_start(
                out=raw[(nm, h)][:, lo:hi, :],
                in_=src[0, h].rearrange("(p t) d -> p t d", t=NT)[:, lo:hi, :],
            )

        def load_mask(i):
            nc.sync.dma_start(out=mb[i][:], in_=mask[0].rearrange("(p t) c -> t p c", t=NT)[i])

        def load_v(h):
            nc.sync.dma_start(out=vraw[h][:], in_=v[0, h].rearrange("(c p) n -> p c n", p=P))

        load_keys("k", k, 0, 0, 4)
        load_keys("pk", pe_k, 0, 0, 4)
        load_queries("q", q, 0, 0, 4)
        load_queries("pq", pe_q, 0, 0, 4)
        load_mask(0)
        load_keys("k", k, 0, 4, 8)
        load_keys("pk", pe_k, 0, 4, 8)
        load_keys("k", k, 0, 8, NT)
        load_keys("pk", pe_k, 0, 8, NT)
        load_mask(1)
        load_queries("q", q, 0, 4, NT)
        load_queries("pq", pe_q, 0, 4, NT)
        load_v(0)
        load_mask(2)
        load_mask(3)
        load_keys("k", k, 1, 0, NT)
        load_keys("pk", pe_k, 1, 0, NT)
        load_mask(4)
        load_queries("q", q, 1, 0, NT)
        load_queries("pq", pe_q, 1, 0, NT)
        load_mask(5)
        load_v(1)
        for i in range(6, NT):
            load_mask(i)

        warm = small.tile([P, 1], F32, tag="warm", name="warm", bufs=1)
        nc.vector.memset(warm[:], 0.0)
        nc.scalar.activation(out=warm[:], in_=warm[:], func=ACT.Exp)

        def bias_from_mask(eng, i, lo, hi):
            eng.tensor_scalar(
                out=mb[i][:, lo:hi], in0=mb[i][:, lo:hi],
                scalar1=-1.0, scalar2=-BIG, op0=ALU.add, op1=ALU.mult,
            )

        vg = {}

        def regroup_v(h):
            vg[h] = gpool.tile([P, NCH, DV, 4], BF16, tag="vg", name="vg", bufs=1, align_bytes=64)
            for g in range(NCH):
                nc.gpsimd.tensor_scalar(
                    out=vg[h][:, g, :, :],
                    in0=vraw[h][:, 4 * g:4 * g + 4, :].rearrange("p t n -> p n t"),
                    scalar1=1.0, scalar2=0.0, op0=ALU.mult, op1=ALU.add,
                )

        def quantise_v(h):
            nc.vector.quantize_mx(
                out=vcodes[h][:].bitcast(FP8X4),
                scales=vscl[h][:],
                in_=vg[h][:].rearrange("p g n t -> p (g n t)"),
            )

        def flip(pool, tag, a, b, h, c, dst, copy):
            bank = pool.tile([P, 8, P], BF16, tag=tag, name="flip")
            for n in range(8):
                src = raw[(a if n < 4 else b, h)]
                nc.tensor.transpose(bank[:, n, :], src[:, 4 * c + n % 4, :], ident[:])
            copy(out=dst, in_=bank[:].rearrange("p (x c) r -> p x (c r)", x=2))

        def flip_keys(pool, tag, h, c, copy):
            flip(pool, tag, "k", "pk", h, c, kk[h][:, :, CH * c:CH * (c + 1)], copy)

        def flip_queries(pool, tag, h, c, copy):
            dst = qq[h][:, :, 4 * c:4 * c + 4, :].rearrange("p x c r -> p x (c r)")
            flip(pool, tag, "q", "pq", h, c, dst, copy)

        st = {}

        def pe_masked(u):
            return u % 4 != 3

        def scores(u):
            h, i = divmod(u, NT)
            banks = []
            for j in range(NCH):
                s = ps_s.tile([P, CH], F32, tag="s", name="s")
                cols = slice(CH * j, CH * (j + 1))
                nc.tensor.matmul(s[:], lhsT=qq[h][:, 0, i, :], rhs=kk[h][:, 0, cols], start=True, stop=False)
                extra = j == NCH - 1 and pe_masked(u)
                nc.tensor.matmul(s[:], lhsT=qq[h][:, 1, i, :], rhs=kk[h][:, 1, cols], start=False, stop=not extra)
                if extra:
                    nc.tensor.matmul(s[:], lhsT=negident[:], rhs=mb[i][:, cols], start=False, stop=True)
                banks.append(s)
            st[("s", u)] = banks

        def mask_and_min(u):
            i = u % NT
            w = wpool.tile([P, L], F32, tag="w", name="w")
            nv = NCH - 1 if pe_masked(u) else NCH
            for j in range(nv):
                cols = slice(CH * j, CH * (j + 1))
                nc.vector.scalar_tensor_tensor(
                    out=w[:, cols], in0=st[("s", u)][j][:], scalar=-SCALE, in1=mb[i][:, cols],
                    op0=ALU.mult, op1=ALU.add,
                )
            wmin = small.tile([P, 1], F32, tag="wmin", name="wmin")
            if pe_masked(u):
                vmin = small.tile([P, 1], F32, tag="vmin", name="vmin")
                nc.vector.tensor_reduce(out=vmin[:], in_=w[:, 0:CH * nv], axis=AX.X, op=ALU.min)
                nc.vector.tensor_scalar(
                    out=w[:, CH * nv:L], in0=st[("s", u)][nv][:], scalar1=-SCALE, scalar2=vmin[:],
                    op0=ALU.mult, op1=ALU.min, accum_out=wmin[:],
                )
            else:
                nc.vector.tensor_reduce(out=wmin[:], in_=w[:], axis=AX.X, op=ALU.min)
            st[("w", u)] = w
            st[("wmin", u)] = wmin

        def pieces(u):
            return 2 if u == NU - 1 else 1

        def exponent(u):
            e = epool.tile([P, L], BF16, tag="e", name="e")
            width = L // pieces(u)
            sums = []
            for a in range(pieces(u)):
                rs = small.tile([P, 1], F32, tag="rs", name="rs")
                cols = slice(a * width, (a + 1) * width)
                nc.scalar.activation(
                    out=e[:, cols], in_=st[("w", u)][:, cols], func=ACT.Exp, bias=st[("wmin", u)][:], scale=-1.0,
                    accum_out=rs[:],
                )
                sums.append(rs)
            st[("e", u)] = e
            st[("rs", u)] = sums

        def flip_e(u):
            e = st[("e", u)]
            banks = []
            for b in range(2):
                xt = ps_x.tile([P, 8, P], BF16, tag="xt", name="xt")
                for n in range(8):
                    c = 8 * b + n
                    nc.tensor.transpose(xt[:, n, :], e[:, P * c:P * (c + 1)], ident[:])
                banks.append(xt)
            st[("xt", u)] = banks

        def group_e(u):
            gr = gpool.tile([P, NCH, P, 4], BF16, tag="gr", name="gr", align_bytes=64)
            for b in range(2):
                copy = nc.vector.tensor_copy if (u >= NU - 2 and b == 0) else nc.scalar.copy
                copy(
                    out=gr[:, 2 * b:2 * b + 2, :, :],
                    in_=st[("xt", u)][b][:].rearrange("p (g t) r -> p g r t", t=4),
                )
            st[("gr", u)] = gr

        def quantise_e(u):
            codes = cpool.tile([P, NCH * P], U32, tag="codes", name="codes", align_bytes=64)
            scl = cpool.tile([P, NCH * P], U8, tag="scl", name="scl", align_bytes=64)
            n = pieces(u)
            for a in range(n):
                words = slice(a * NCH * P // n, (a + 1) * NCH * P // n)
                nc.vector.quantize_mx(
                    out=codes[:, words].bitcast(FP8X4), scales=scl[:, words],
                    in_=st[("gr", u)][:, a * NCH // n:(a + 1) * NCH // n, :, :].rearrange("p g r t -> p (g r t)"),
                )
            rinv = small.tile([P, 1], F32, tag="rinv", name="rinv")
            sums = st[("rs", u)]
            if n == 2:
                nc.vector.tensor_tensor(out=sums[0][:], in0=sums[0][:], in1=sums[1][:], op=ALU.add)
            nc.vector.reciprocal(rinv[:], sums[0][:])
            st[("codes", u)] = codes
            st[("scl", u)] = scl
            st[("rinv", u)] = rinv

        def weighted_sum(u):
            h, i = divmod(u, NT)
            o = ps_o.tile([P, DV], F32, tag="o", name="o")
            for g in range(NCH):
                nc.tensor.matmul_mx(
                    out=o[:],
                    lhsT=st[("codes", u)][:, P * g:P * (g + 1)].bitcast(FP8X4),
                    lhsT_scale=st[("scl", u)][:, P * g:P * (g + 1)],
                    rhs=vcodes[h][:, DV * g:DV * (g + 1)].bitcast(FP8X4),
                    rhs_scale=vscl[h][:, DV * g:DV * (g + 1)],
                    start=(g == 0), stop=(g == NCH - 1),
                )
            st[("o", u)] = o

        def on_vector(u):
            return pe_masked(u) and u < NU - 3

        def finish(u):
            h, i = divmod(u, NT)
            o = st[("o", u)]
            res = opool.tile([P, DV], F32, tag="res", name="res")
            if u >= NU - 3 or on_vector(u):
                nc.vector.tensor_scalar_mul(out=res[:], in0=o[:], scalar1=st[("rinv", u)][:])
            else:
                nc.scalar.activation(out=res[:], in_=o[:], func=ACT.Copy, scale=st[("rinv", u)][:])
            nc.sync.dma_start(out=out[0, h].rearrange("(p t) n -> t p n", t=NT)[i], in_=res[:])

        vcopy = nc.vector.tensor_copy
        scopy = nc.scalar.copy
        flip_queries(ps_x, "xt", 0, 0, vcopy)
        flip_keys(ps_s, "s", 0, 0, scopy)
        for j in range(NCH):
            bias_from_mask(nc.vector, 0, CH * j, CH * (j + 1))
        flip_keys(ps_s, "s", 0, 1, vcopy)
        flip_keys(ps_s, "s", 0, 2, scopy)
        flip_keys(ps_s, "s", 0, 3, vcopy)
        scores(0)
        for c in range(1, 4):
            flip_queries(ps_p, "p", 0, c, scopy)

        bias_from_mask(nc.gpsimd, 1, 0, L)
        regroup_v(0)
        for i in range(2, 7):
            bias_from_mask(nc.gpsimd, i, 0, L)

        later = {}
        for c in range(4):
            later[3 + c] = ("k", c)
            later[7 + c] = ("q", c)

        for s in range(NU + 2):
            if s < NU:
                mask_and_min(s)
            if s >= 3 and on_vector(s - 3):
                finish(s - 3)
            if s + 1 < NU:
                scores(s + 1)
            if 1 <= s <= NU:
                flip_e(s - 1)
            if s < NU:
                exponent(s)
            if 1 <= s <= NU:
                group_e(s - 1)
            if s == 1:
                quantise_v(0)
            if s == 2:
                regroup_v(1)
                for i in range(7, NT):
                    bias_from_mask(nc.gpsimd, i, 0, L)
            if s == 12:
                quantise_v(1)
            if s >= 2:
                quantise_e(s - 2)
                weighted_sum(s - 2)
                if not on_vector(s - 2):
                    finish(s - 2)
            if s in later:
                kind, c = later[s]
                if kind == "k":
                    flip_keys(ps_p, "p", 1, c, vcopy)
                else:
                    flip_queries(ps_p, "p", 1, c, vcopy)
